import numpy as np
import ml_dtypes


def mxq(x, axis, fmt="e4m3"):
    dtype, down = {"e4m3": (ml_dtypes.float8_e4m3fn, 7), "e5m2": (ml_dtypes.float8_e5m2, 14)}[fmt]
    v = np.moveaxis(np.asarray(x, np.float32).astype(ml_dtypes.bfloat16).astype(np.float64), axis, -1)
    blocks = v.reshape(v.shape[:-1] + (-1, 32))
    amax = np.abs(blocks).max(-1, keepdims=True)
    byte = np.maximum(np.where(amax > 0, np.frexp(amax)[1] - 1 + 127, 0) - down, 1)
    scale = np.exp2(byte - 127.0)
    codes = (blocks / scale).astype(np.float32).astype(dtype).astype(np.float64)
    return np.moveaxis((codes * scale).reshape(v.shape), -1, axis)


WIDE = False


def mx_kscale(k):
    if not WIDE:
        return np.ones(k)
    levels = np.array([10, -10, 5, -5, 0])
    a = np.random.permutation(np.resize(levels, k // 512 * 4)).reshape(k // 512, 4)
    idx = np.arange(k)
    return np.exp2(a[idx // 512, idx % 128 // 32])


BF16 = ml_dtypes.bfloat16


def bf(x):
    return np.asarray(x, np.float32).astype(BF16)


def f64(x):
    return np.asarray(x).astype(np.float64)


B, T, E, H, DC, KB, DFF = 16, 512, 512, 8, 1, 512, 4096
HD = E // H
HALF = H // 2


def mix_matrices(mix_w, decay):
    i = np.arange(T)[:, None]
    j = np.arange(T)[None, :]
    d = np.clip(decay, 0.9, 1.0)
    expo = (j - i) / DC
    dec = d[:, None, None] ** expo
    causal = j >= i
    mcol = np.where(causal, mix_w[:HALF, None, :] * dec[:HALF], 0.0)
    mrow = np.where(causal, mix_w[HALF:, :, None] * dec[HALF:], 0.0)
    return np.concatenate([mcol, mrow], axis=0)


def setup_inputs():
    s = mx_kscale(T)
    u = mx_kscale(E)[::HD]
    st = np.concatenate([np.ones((HALF, T)), np.tile(s, (HALF, 1))], axis=0)
    return {"p": bf(np.random.standard_normal((B, H, T, HD)) / st[None, :, :, None]),
            "mix_w": bf(np.random.standard_normal((H, T)) * 3.0 / np.sqrt(T) * st * u[:, None]),
            "mix_b": bf(np.random.standard_normal((H, T)) * 0.2 * u[:, None]),
            "decay": bf(np.random.permutation(np.linspace(0.8, 1.04, H))),
            "out_w": bf(np.random.standard_normal((E, E)) / np.sqrt(E) / np.repeat(u, HD)[:, None]),
            "out_b": bf(np.random.standard_normal(E) * 0.2),
            "x": bf(np.random.standard_normal((B, T, E)))}


def reference(p, mix_w, mix_b, decay, out_w, out_b, x):
    m = mix_matrices(f64(mix_w), f64(decay))
    pq = mxq(f64(p), 2, "e4m3")
    cols = []
    for s0 in range(0, T, KB):
        s1 = s0 + KB
        mq = mxq(m[:, :s1, s0:s1], 1, "e4m3")
        cols.append(mq.transpose(0, 2, 1) @ pq[:, :, :s1, :])
    mixed = np.concatenate(cols, axis=2) + f64(mix_b)[None, :, :, None]
    c = mixed.transpose(0, 2, 1, 3).reshape(B, T, E)
    y = (mxq(c, 2, "e4m3") @ mxq(f64(out_w), 0, "e4m3")) + f64(out_b)
    return y + f64(x)

@@ -1,0 +1,245 @@
+from contextlib import ExitStack
+
+import concourse.mybir as mybir
+
+F32 = mybir.dt.float32
+BF16 = mybir.dt.bfloat16
+I32 = mybir.dt.int32
+U32 = mybir.dt.uint32
+U8 = mybir.dt.uint8
+FP8X4 = mybir.dt.float8_e4m3fn_x4
+ALU = mybir.AluOpType
+ACT = mybir.ActivationFunctionType
+
+B, H, T, HD = 16, 8, 512, 64
+E = H * HD
+HALF = H // 2
+P = 128
+PACK = 4
+PAIR = 2
+N_PAIRS = B // PAIR
+PARITIES = 2
+S_TILE = 128
+N_S_TILES = T // S_TILE
+
+FLOPS = 2 * B * H * T * T * HD + 2 * B * T * E * E
+
+
+def tile_mixerblock_pa_t_kernel(tc, p, mix_w, mix_b, decay, out_w, out_b, x, out):
+    nc = tc.nc
+    with ExitStack() as ctx:
+        const = ctx.enter_context(tc.tile_pool(name="const", bufs=1))
+        build = ctx.enter_context(tc.tile_pool(name="build", bufs=2))
+        stream = ctx.enter_context(tc.tile_pool(name="stream", bufs=2))
+        c_psum = ctx.enter_context(tc.psum_pool(name="c_psum", bufs=4))
+        y_psum = ctx.enter_context(tc.psum_pool(name="y_psum", bufs=4))
+
+        def load_pair(bp):
+            p_raw = stream.tile([P, PAIR, H, PACK * HD], BF16, name="p_raw")
+            x_rows = stream.tile([P, PAIR, N_S_TILES, E], BF16, name="x_rows")
+            for b2 in range(PAIR):
+                b = PAIR * bp + b2
+                nc.sync.dma_start(out=p_raw[:, b2], in_=p[b].rearrange("h (q j) f -> q h (j f)", j=PACK))
+            for b2 in range(PAIR):
+                b = PAIR * bp + b2
+                nc.sync.dma_start(out=x_rows[:, b2], in_=x[b].rearrange("(i r) n -> r i n", r=S_TILE))
+            return p_raw, x_rows
+
+        loaded = {0: load_pair(0)}
+
+        decay_raw = const.tile([P, H], BF16)
+        nc.sync.dma_start(out=decay_raw[:], in_=decay.partition_broadcast(P))
+        w_rows = const.tile([P, HALF, PACK], BF16)
+        with nc.allow_non_contiguous_dma(reason="four neighbouring weights to a partition, once"):
+            nc.sync.dma_start(out=w_rows[:], in_=mix_w[HALF:H, :].rearrange("h (q j) -> q h j", j=PACK))
+        w_cols = const.tile([P, HALF, T], BF16)
+        nc.sync.dma_start(
+            out=w_cols[:].rearrange("q h s -> q (h s)"),
+            in_=mix_w[0:HALF, :].rearrange("h s -> (h s)").partition_broadcast(P),
+        )
+
+        s_int = const.tile([P, T], I32)
+        nc.gpsimd.iota(s_int[:], pattern=[[1, T]], base=0, channel_multiplier=0)
+        t_int = const.tile([P, PACK], I32)
+        nc.gpsimd.iota(t_int[:], pattern=[[1, PACK]], base=0, channel_multiplier=PACK)
+        s_idx = const.tile([P, T], F32)
+        nc.vector.tensor_copy(out=s_idx[:], in_=s_int[:])
+        t_idx = const.tile([P, PACK], F32)
+        nc.vector.tensor_copy(out=t_idx[:], in_=t_int[:])
+
+        d = const.tile([P, H], F32)
+        nc.vector.tensor_scalar(out=d[:], in0=decay_raw[:], scalar1=0.9, scalar2=1.0, op0=ALU.max, op1=ALU.min)
+        ln_d = const.tile([P, H], F32)
+        nc.scalar.activation(out=ln_d[:], in_=d[:], func=ACT.Ln)
+
+        row_arg = const.tile([P, H, PACK], F32)
+        nc.vector.tensor_tensor(
+            out=row_arg[:],
+            in0=t_idx[:].unsqueeze(1).to_broadcast([P, H, PACK]),
+            in1=ln_d[:].unsqueeze(2).to_broadcast([P, H, PACK]),
+            op=ALU.mult,
+        )
+        row_fac = const.tile([P, H, PACK], F32)
+        nc.scalar.activation(out=row_fac[:], in_=row_arg[:], func=ACT.Exp, scale=-1.0)
+        nc.vector.tensor_tensor(out=row_fac[:, HALF:H, :], in0=row_fac[:, HALF:H, :], in1=w_rows[:], op=ALU.mult)
+
+        col_fac = const.tile([P, H, T], F32)
+        for h in range(H):
+            nc.scalar.activation(out=col_fac[:, h, :], in_=s_idx[:], func=ACT.Exp, scale=ln_d[:, h : h + 1])
+        nc.vector.tensor_tensor(out=col_fac[:, 0:HALF, :], in0=col_fac[:, 0:HALF, :], in1=w_cols[:], op=ALU.mult)
+
+        m_codes = const.tile([P, H, T], U32, align_bytes=64)
+        m_scales = const.tile([P, H, T], U8, align_bytes=64)
+        for h in [PARITIES * j + g for g in range(PARITIES) for j in range(H // PARITIES)]:
+            masked = build.tile([P, T, PACK], F32)
+            nc.scalar.copy(out=masked[:], in_=col_fac[:, h, :].unsqueeze(2).to_broadcast([P, T, PACK]))
+            nc.gpsimd.affine_select(
+                out=masked[:],
+                in_=masked[:],
+                pattern=[[1, T], [-1, PACK]],
+                compare_op=ALU.is_ge,
+                fill=0.0,
+                base=0,
+                channel_multiplier=-PACK,
+            )
+            m_grouped = build.tile([P, T, PACK], BF16, align_bytes=64)
+            nc.vector.tensor_tensor(
+                out=m_grouped[:],
+                in0=masked[:],
+                in1=row_fac[:, h, :].unsqueeze(1).to_broadcast([P, T, PACK]),
+                op=ALU.mult,
+            )
+            nc.vector.quantize_mx(
+                out=m_codes[:, h, :].bitcast(FP8X4),
+                scales=m_scales[:, h, :],
+                in_=m_grouped[:].rearrange("q s j -> q (s j)"),
+            )
+
+        w_raw = const.tile([P, PARITIES, PACK, E], BF16)
+        for b2 in range(PAIR):
+            for g in range(PARITIES):
+                nc.sync.dma_start(
+                    out=w_raw[b2 * HD : (b2 + 1) * HD, g],
+                    in_=out_w.rearrange("(j g f) n -> g f j n", g=PARITIES, f=HD)[g],
+                )
+        w_codes = []
+        w_scales = []
+        for b2 in range(PAIR):
+            own = slice(b2 * HD, (b2 + 1) * HD)
+            other = slice((1 - b2) * HD, (2 - b2) * HD)
+            w_grouped = const.tile([P, PARITIES, E, PACK], BF16, align_bytes=64, name="w_grouped%d" % b2)
+            nc.vector.memset(w_grouped[other], 0.0)
+            nc.vector.tensor_copy(out=w_grouped[own], in_=w_raw[own].rearrange("q g j n -> q g n j"))
+            codes = const.tile([P, PARITIES, E], U32, align_bytes=64, name="w_codes%d" % b2)
+            scales = const.tile([P, PARITIES, E], U8, align_bytes=64, name="w_scales%d" % b2)
+            for g in range(PARITIES):
+                nc.vector.quantize_mx(
+                    out=codes[:, g, :].bitcast(FP8X4),
+                    scales=scales[:, g, :],
+                    in_=w_grouped[:, g].rearrange("q n j -> q (n j)"),
+                )
+            w_codes.append(codes)
+            w_scales.append(scales)
+
+        mix_b_all = const.tile([P, H, T], BF16)
+        nc.sync.dma_start(
+            out=mix_b_all[:].rearrange("q h s -> q (h s)"),
+            in_=mix_b.rearrange("h s -> (h s)").partition_broadcast(P),
+        )
+        out_b_all = const.tile([P, E], BF16)
+        nc.sync.dma_start(out=out_b_all[:], in_=out_b.partition_broadcast(P))
+
+        def prepare_pair(p_raw, x_rows):
+            p_grouped = stream.tile([P, H, PAIR, HD, PACK], BF16, align_bytes=64, name="p_grouped")
+            for b2 in range(PAIR):
+                nc.scalar.copy(
+                    out=p_grouped[:, :, b2, :, :],
+                    in_=p_raw[:, b2].rearrange("q h (j f) -> q h f j", j=PACK),
+                )
+            p_codes = stream.tile([P, H * PAIR * HD], U32, align_bytes=64, name="p_codes")
+            p_scales = stream.tile([P, H * PAIR * HD], U8, align_bytes=64, name="p_scales")
+            nc.vector.quantize_mx(
+                out=p_codes[:].bitcast(FP8X4),
+                scales=p_scales[:],
+                in_=p_grouped[:].rearrange("q h b f j -> q (h b f j)"),
+            )
+            resid = stream.tile([P, PAIR, N_S_TILES, E], F32, name="resid")
+            for b2 in range(PAIR):
+                nc.gpsimd.tensor_tensor(
+                    out=resid[:, b2],
+                    in0=x_rows[:, b2],
+                    in1=out_b_all[:].unsqueeze(1).to_broadcast([P, N_S_TILES, E]),
+                    op=ALU.add,
+                )
+            return p_codes, p_scales, resid
+
+        def mix_pair(p_codes, p_scales):
+            c_grouped = []
+            for g in range(PARITIES):
+                grouped = stream.tile([P, T, PACK], BF16, align_bytes=64, name="c_grouped%d" % g)
+                for i in range(N_S_TILES):
+                    s_cols = slice(i * S_TILE, (i + 1) * S_TILE)
+                    mixed = c_psum.tile([P, PACK, S_TILE], F32, name="mixed")
+                    for j in range(PACK):
+                        h = PARITIES * j + g
+                        h_cols = slice(h * PAIR * HD, (h + 1) * PAIR * HD)
+                        nc.tensor.matmul_mx(
+                            out=mixed[:, j, :],
+                            lhsT=p_codes[:, h_cols].bitcast(FP8X4),
+                            lhsT_scale=p_scales[:, h_cols],
+                            rhs=m_codes[:, h, s_cols].bitcast(FP8X4),
+                            rhs_scale=m_scales[:, h, s_cols],
+                            start=True,
+                            stop=True,
+                        )
+                    nc.vector.tensor_tensor(
+                        out=grouped[:, s_cols, :],
+                        in0=mixed[:].rearrange("q j s -> q s j"),
+                        in1=mix_b_all[:, g:H:PARITIES, s_cols].rearrange("q j s -> q s j"),
+                        op=ALU.add,
+                    )
+                c_grouped.append(grouped)
+            c_codes = []
+            c_scales = []
+            for g in range(PARITIES):
+                codes = stream.tile([P, T], U32, align_bytes=64, name="c_codes%d" % g)
+                scales = stream.tile([P, T], U8, align_bytes=64, name="c_scales%d" % g)
+                nc.vector.quantize_mx(
+                    out=codes[:].bitcast(FP8X4),
+                    scales=scales[:],
+                    in_=c_grouped[g][:].rearrange("q s j -> q (s j)"),
+                )
+                c_codes.append(codes)
+                c_scales.append(scales)
+            return c_codes, c_scales
+
+        def project_pair(bp, c_codes, c_scales, resid):
+            for b2 in range(PAIR):
+                for i in range(N_S_TILES):
+                    s_cols = slice(i * S_TILE, (i + 1) * S_TILE)
+                    y = y_psum.tile([P, E], F32, name="y")
+                    for g in range(PARITIES):
+                        nc.tensor.matmul_mx(
+                            out=y[:],
+                            lhsT=c_codes[g][:, s_cols].bitcast(FP8X4),
+                            lhsT_scale=c_scales[g][:, s_cols],
+                            rhs=w_codes[b2][:, g, :].bitcast(FP8X4),
+                            rhs_scale=w_scales[b2][:, g, :],
+                            start=(g == 0),
+                            stop=(g == PARITIES - 1),
+                        )
+                    nc.vector.tensor_tensor(out=resid[:, b2, i, :], in0=y[:], in1=resid[:, b2, i, :], op=ALU.add)
+                nc.sync.dma_start(
+                    out=out[PAIR * bp + b2].rearrange("(i r) n -> r i n", r=S_TILE),
+                    in_=resid[:, b2],
+                )
+
+        prepared = {0: prepare_pair(*loaded[0])}
+        for bp in range(N_PAIRS):
+            if bp + 1 < N_PAIRS:
+                loaded[bp + 1] = load_pair(bp + 1)
+            p_codes, p_scales, resid = prepared[bp]
+            c_codes, c_scales = mix_pair(p_codes, p_scales)
+            if bp + 1 < N_PAIRS:
+                prepared[bp + 1] = prepare_pair(*loaded[bp + 1])
+            project_pair(bp, c_codes, c_scales, resid)

@@ -165,7 +165,7 @@ def tile_mixerblock_pa_t_kernel(tc, p, mix_w, mix_b, decay, out_w, out_b, x, out
             )
             resid = stream.tile([P, PAIR, N_S_TILES, E], F32, name="resid")
             for b2 in range(PAIR):
-                nc.gpsimd.tensor_tensor(
+                nc.vector.tensor_tensor(
                     out=resid[:, b2],
                     in0=x_rows[:, b2],
                     in1=out_b_all[:].unsqueeze(1).to_broadcast([P, N_S_TILES, E]),

@@ -1,6 +1,7 @@
 from contextlib import ExitStack
 
 import concourse.mybir as mybir
+from concourse.masks import make_identity
 
 F32 = mybir.dt.float32
 BF16 = mybir.dt.bfloat16
@@ -19,8 +20,9 @@ PACK = 4
 PAIR = 2
 N_PAIRS = B // PAIR
 PARITIES = 2
-S_TILE = 128
-N_S_TILES = T // S_TILE
+TILE = 128
+N_TILES = T // TILE
+STEPS = PAIR * N_TILES
 
 FLOPS = 2 * B * H * T * T * HD + 2 * B * T * E * E
 
@@ -29,217 +31,254 @@ def tile_mixerblock_pa_t_kernel(tc, p, mix_w, mix_b, decay, out_w, out_b, x, out
     nc = tc.nc
     with ExitStack() as ctx:
         const = ctx.enter_context(tc.tile_pool(name="const", bufs=1))
-        build = ctx.enter_context(tc.tile_pool(name="build", bufs=2))
         stream = ctx.enter_context(tc.tile_pool(name="stream", bufs=2))
-        c_psum = ctx.enter_context(tc.psum_pool(name="c_psum", bufs=4))
-        y_psum = ctx.enter_context(tc.psum_pool(name="y_psum", bufs=4))
+        psum = ctx.enter_context(tc.psum_pool(name="psum", bufs=2))
 
-        def load_pair(bp):
-            p_raw = stream.tile([P, PAIR, H, PACK * HD], BF16, name="p_raw")
-            x_rows = stream.tile([P, PAIR, N_S_TILES, E], BF16, name="x_rows")
-            for b2 in range(PAIR):
-                b = PAIR * bp + b2
-                nc.sync.dma_start(out=p_raw[:, b2], in_=p[b].rearrange("h (q j) f -> q h (j f)", j=PACK))
-            for b2 in range(PAIR):
-                b = PAIR * bp + b2
-                nc.sync.dma_start(out=x_rows[:, b2], in_=x[b].rearrange("(i r) n -> r i n", r=S_TILE))
-            return p_raw, x_rows
+        p_raw, x_rows, p_grouped, p_mx, c_grouped, c_mx, y_t, y_rows = {}, {}, {}, {}, {}, {}, {}, {}
 
-        loaded = {0: load_pair(0)}
+        def load_p(bp):
+            p_raw[bp] = stream.tile([P, PAIR, H, PACK * HD], BF16, name="p_raw")
+            for b2 in range(PAIR):
+                nc.sync.dma_start(
+                    out=p_raw[bp][:, b2], in_=p[PAIR * bp + b2].rearrange("h (q j) f -> q h (j f)", j=PACK)
+                )
+
+        def load_x(bp):
+            x_rows[bp] = stream.tile([P, PAIR, N_TILES, E], BF16, name="x_rows", bufs=3)
+            for b2 in range(PAIR):
+                nc.sync.dma_start(
+                    out=x_rows[bp][:, b2], in_=x[PAIR * bp + b2].rearrange("(i r) n -> r i n", r=TILE)
+                )
+
+        load_p(0)
 
         decay_raw = const.tile([P, H], BF16)
         nc.sync.dma_start(out=decay_raw[:], in_=decay.partition_broadcast(P))
         w_rows = const.tile([P, HALF, PACK], BF16)
-        with nc.allow_non_contiguous_dma(reason="four neighbouring weights to a partition, once"):
+        out_b_raw = const.tile([P, N_TILES], BF16)
+        with nc.allow_non_contiguous_dma(reason="two small vectors, spread over the partitions once"):
             nc.sync.dma_start(out=w_rows[:], in_=mix_w[HALF:H, :].rearrange("h (q j) -> q h j", j=PACK))
-        w_cols = const.tile([P, HALF, T], BF16)
-        nc.sync.dma_start(
-            out=w_cols[:].rearrange("q h s -> q (h s)"),
-            in_=mix_w[0:HALF, :].rearrange("h s -> (h s)").partition_broadcast(P),
-        )
-
-        s_int = const.tile([P, T], I32)
-        nc.gpsimd.iota(s_int[:], pattern=[[1, T]], base=0, channel_multiplier=0)
-        t_int = const.tile([P, PACK], I32)
-        nc.gpsimd.iota(t_int[:], pattern=[[1, PACK]], base=0, channel_multiplier=PACK)
-        s_idx = const.tile([P, T], F32)
-        nc.vector.tensor_copy(out=s_idx[:], in_=s_int[:])
-        t_idx = const.tile([P, PACK], F32)
-        nc.vector.tensor_copy(out=t_idx[:], in_=t_int[:])
-
-        d = const.tile([P, H], F32)
-        nc.vector.tensor_scalar(out=d[:], in0=decay_raw[:], scalar1=0.9, scalar2=1.0, op0=ALU.max, op1=ALU.min)
-        ln_d = const.tile([P, H], F32)
-        nc.scalar.activation(out=ln_d[:], in_=d[:], func=ACT.Ln)
-
-        row_arg = const.tile([P, H, PACK], F32)
-        nc.vector.tensor_tensor(
-            out=row_arg[:],
-            in0=t_idx[:].unsqueeze(1).to_broadcast([P, H, PACK]),
-            in1=ln_d[:].unsqueeze(2).to_broadcast([P, H, PACK]),
-            op=ALU.mult,
-        )
-        row_fac = const.tile([P, H, PACK], F32)
-        nc.scalar.activation(out=row_fac[:], in_=row_arg[:], func=ACT.Exp, scale=-1.0)
-        nc.vector.tensor_tensor(out=row_fac[:, HALF:H, :], in0=row_fac[:, HALF:H, :], in1=w_rows[:], op=ALU.mult)
-
-        col_fac = const.tile([P, H, T], F32)
-        for h in range(H):
-            nc.scalar.activation(out=col_fac[:, h, :], in_=s_idx[:], func=ACT.Exp, scale=ln_d[:, h : h + 1])
-        nc.vector.tensor_tensor(out=col_fac[:, 0:HALF, :], in0=col_fac[:, 0:HALF, :], in1=w_cols[:], op=ALU.mult)
+            nc.sync.dma_start(out=out_b_raw[:], in_=out_b.rearrange("(k n) -> n k", n=TILE))
+        out_b_col = const.tile([P, N_TILES], F32)
+        nc.vector.tensor_copy(out=out_b_col[:], in_=out_b_raw[:])
+        mix_b_all = const.tile([P, H, T], BF16)
+        identity = const.tile([P, P], F32)
+        make_identity(nc, identity[:])
 
         m_codes = const.tile([P, H, T], U32, align_bytes=64)
         m_scales = const.tile([P, H, T], U8, align_bytes=64)
-        for h in [PARITIES * j + g for g in range(PARITIES) for j in range(H // PARITIES)]:
-            masked = build.tile([P, T, PACK], F32)
-            nc.scalar.copy(out=masked[:], in_=col_fac[:, h, :].unsqueeze(2).to_broadcast([P, T, PACK]))
+        w_codes = [const.tile([P, PARITIES, E], U32, align_bytes=64, name="w_codes%d" % b2) for b2 in range(PAIR)]
+        w_scales = [const.tile([P, PARITIES, E], U8, align_bytes=64, name="w_scales%d" % b2) for b2 in range(PAIR)]
+
+        def regroup_head(bp, h):
+            if h == 0:
+                p_grouped[bp] = stream.tile([P, H, PAIR, HD, PACK], BF16, align_bytes=64, name="p_grouped")
+            nc.scalar.copy(
+                out=p_grouped[bp][:, h],
+                in_=p_raw[bp][:, :, h, :].rearrange("q b (j f) -> q b f j", j=PACK),
+            )
+
+        def quantise_p(bp):
+            codes = stream.tile([P, H * PAIR * HD], U32, align_bytes=64, name="p_codes")
+            scales = stream.tile([P, H * PAIR * HD], U8, align_bytes=64, name="p_scales")
+            nc.vector.quantize_mx(
+                out=codes[:].bitcast(FP8X4),
+                scales=scales[:],
+                in_=p_grouped[bp][:].rearrange("q h b f j -> q (h b f j)"),
+            )
+            p_mx[bp] = (codes, scales)
+
+        with tc.tile_pool(name="setup", bufs=1) as setup:
+            w_cols = setup.tile([P, HALF, T], BF16)
+            nc.sync.dma_start(
+                out=w_cols[:].rearrange("q h s -> q (h s)"),
+                in_=mix_w[0:HALF, :].rearrange("h s -> (h s)").partition_broadcast(P),
+            )
+            w_raw = setup.tile([P, PARITIES, PACK, E], BF16)
+            for b2 in range(PAIR):
+                for g in range(PARITIES):
+                    nc.sync.dma_start(
+                        out=w_raw[b2 * HD : (b2 + 1) * HD, g],
+                        in_=out_w.rearrange("(j g f) n -> g f j n", g=PARITIES, f=HD)[g],
+                    )
+            nc.sync.dma_start(
+                out=mix_b_all[:].rearrange("q h s -> q (h s)"),
+                in_=mix_b.rearrange("h s -> (h s)").partition_broadcast(P),
+            )
+            load_p(1)
+
+            s_int = setup.tile([P, T], I32)
+            nc.gpsimd.iota(s_int[:], pattern=[[1, T]], base=0, channel_multiplier=0)
+            t_int = setup.tile([P, PACK], I32)
+            nc.gpsimd.iota(t_int[:], pattern=[[1, PACK]], base=0, channel_multiplier=PACK)
+            causal = setup.tile([P, PACK, T], F32)
+            nc.gpsimd.memset(causal[:], 1.0)
             nc.gpsimd.affine_select(
-                out=masked[:],
-                in_=masked[:],
-                pattern=[[1, T], [-1, PACK]],
+                out=causal[:],
+                in_=causal[:],
+                pattern=[[-1, PACK], [1, T]],
                 compare_op=ALU.is_ge,
                 fill=0.0,
                 base=0,
                 channel_multiplier=-PACK,
             )
-            m_grouped = build.tile([P, T, PACK], BF16, align_bytes=64)
+            s_idx = setup.tile([P, T], F32)
+            nc.vector.tensor_copy(out=s_idx[:], in_=s_int[:])
+            t_idx = setup.tile([P, PACK], F32)
+            nc.vector.tensor_copy(out=t_idx[:], in_=t_int[:])
+
+            d = setup.tile([P, H], F32)
+            nc.vector.tensor_scalar(
+                out=d[:], in0=decay_raw[:], scalar1=0.9, scalar2=1.0, op0=ALU.max, op1=ALU.min
+            )
+            ln_d = setup.tile([P, H], F32)
+            nc.scalar.activation(out=ln_d[:], in_=d[:], func=ACT.Ln)
+
+            row_arg = setup.tile([P, H, PACK], F32)
             nc.vector.tensor_tensor(
-                out=m_grouped[:],
-                in0=masked[:],
-                in1=row_fac[:, h, :].unsqueeze(1).to_broadcast([P, T, PACK]),
+                out=row_arg[:],
+                in0=t_idx[:].unsqueeze(1).to_broadcast([P, H, PACK]),
+                in1=ln_d[:].unsqueeze(2).to_broadcast([P, H, PACK]),
                 op=ALU.mult,
             )
-            nc.vector.quantize_mx(
-                out=m_codes[:, h, :].bitcast(FP8X4),
-                scales=m_scales[:, h, :],
-                in_=m_grouped[:].rearrange("q s j -> q (s j)"),
+            row_fac = setup.tile([P, H, PACK], F32)
+            nc.scalar.activation(out=row_fac[:], in_=row_arg[:], func=ACT.Exp, scale=-1.0)
+            nc.vector.tensor_tensor(
+                out=row_fac[:, HALF:H, :], in0=row_fac[:, HALF:H, :], in1=w_rows[:], op=ALU.mult
             )
 
-        w_raw = const.tile([P, PARITIES, PACK, E], BF16)
-        for b2 in range(PAIR):
-            for g in range(PARITIES):
-                nc.sync.dma_start(
-                    out=w_raw[b2 * HD : (b2 + 1) * HD, g],
-                    in_=out_w.rearrange("(j g f) n -> g f j n", g=PARITIES, f=HD)[g],
-                )
-        w_codes = []
-        w_scales = []
-        for b2 in range(PAIR):
-            own = slice(b2 * HD, (b2 + 1) * HD)
-            other = slice((1 - b2) * HD, (2 - b2) * HD)
-            w_grouped = const.tile([P, PARITIES, E, PACK], BF16, align_bytes=64, name="w_grouped%d" % b2)
-            nc.vector.memset(w_grouped[other], 0.0)
-            nc.vector.tensor_copy(out=w_grouped[own], in_=w_raw[own].rearrange("q g j n -> q g n j"))
-            codes = const.tile([P, PARITIES, E], U32, align_bytes=64, name="w_codes%d" % b2)
-            scales = const.tile([P, PARITIES, E], U8, align_bytes=64, name="w_scales%d" % b2)
-            for g in range(PARITIES):
-                nc.vector.quantize_mx(
-                    out=codes[:, g, :].bitcast(FP8X4),
-                    scales=scales[:, g, :],
-                    in_=w_grouped[:, g].rearrange("q n j -> q (n j)"),
-                )
-            w_codes.append(codes)
-            w_scales.append(scales)
-
-        mix_b_all = const.tile([P, H, T], BF16)
-        nc.sync.dma_start(
-            out=mix_b_all[:].rearrange("q h s -> q (h s)"),
-            in_=mix_b.rearrange("h s -> (h s)").partition_broadcast(P),
-        )
-        out_b_all = const.tile([P, E], BF16)
-        nc.sync.dma_start(out=out_b_all[:], in_=out_b.partition_broadcast(P))
-
-        def prepare_pair(p_raw, x_rows):
-            p_grouped = stream.tile([P, H, PAIR, HD, PACK], BF16, align_bytes=64, name="p_grouped")
-            for b2 in range(PAIR):
-                nc.scalar.copy(
-                    out=p_grouped[:, :, b2, :, :],
-                    in_=p_raw[:, b2].rearrange("q h (j f) -> q h f j", j=PACK),
-                )
-            p_codes = stream.tile([P, H * PAIR * HD], U32, align_bytes=64, name="p_codes")
-            p_scales = stream.tile([P, H * PAIR * HD], U8, align_bytes=64, name="p_scales")
-            nc.vector.quantize_mx(
-                out=p_codes[:].bitcast(FP8X4),
-                scales=p_scales[:],
-                in_=p_grouped[:].rearrange("q h b f j -> q (h b f j)"),
+            col_fac = setup.tile([P, H, T], F32)
+            for h in range(H):
+                nc.scalar.activation(out=col_fac[:, h, :], in_=s_idx[:], func=ACT.Exp, scale=ln_d[:, h : h + 1])
+            nc.vector.tensor_tensor(
+                out=col_fac[:, 0:HALF, :], in0=col_fac[:, 0:HALF, :], in1=w_cols[:], op=ALU.mult
             )
-            resid = stream.tile([P, PAIR, N_S_TILES, E], F32, name="resid")
-            for b2 in range(PAIR):
-                nc.vector.tensor_tensor(
-                    out=resid[:, b2],
-                    in0=x_rows[:, b2],
-                    in1=out_b_all[:].unsqueeze(1).to_broadcast([P, N_S_TILES, E]),
-                    op=ALU.add,
-                )
-            return p_codes, p_scales, resid
 
-        def mix_pair(p_codes, p_scales):
-            c_grouped = []
             for g in range(PARITIES):
-                grouped = stream.tile([P, T, PACK], BF16, align_bytes=64, name="c_grouped%d" % g)
-                for i in range(N_S_TILES):
-                    s_cols = slice(i * S_TILE, (i + 1) * S_TILE)
-                    mixed = c_psum.tile([P, PACK, S_TILE], F32, name="mixed")
+                for h in range(g, H, PARITIES):
+                    row_masked = setup.tile([P, PACK, T], F32, name="row_masked", bufs=2)
                     for j in range(PACK):
-                        h = PARITIES * j + g
-                        h_cols = slice(h * PAIR * HD, (h + 1) * PAIR * HD)
-                        nc.tensor.matmul_mx(
-                            out=mixed[:, j, :],
-                            lhsT=p_codes[:, h_cols].bitcast(FP8X4),
-                            lhsT_scale=p_scales[:, h_cols],
-                            rhs=m_codes[:, h, s_cols].bitcast(FP8X4),
-                            rhs_scale=m_scales[:, h, s_cols],
-                            start=True,
-                            stop=True,
+                        nc.scalar.activation(
+                            out=row_masked[:, j, :], in_=causal[:, j, :], func=ACT.Copy, scale=row_fac[:, h, j : j + 1]
                         )
+                    m_grouped = setup.tile([P, T, PACK], BF16, align_bytes=64, name="m_grouped", bufs=2)
                     nc.vector.tensor_tensor(
-                        out=grouped[:, s_cols, :],
-                        in0=mixed[:].rearrange("q j s -> q s j"),
-                        in1=mix_b_all[:, g:H:PARITIES, s_cols].rearrange("q j s -> q s j"),
-                        op=ALU.add,
+                        out=m_grouped[:],
+                        in0=row_masked[:].rearrange("q j s -> q s j"),
+                        in1=col_fac[:, h, :].unsqueeze(2).to_broadcast([P, T, PACK]),
+                        op=ALU.mult,
                     )
-                c_grouped.append(grouped)
-            c_codes = []
-            c_scales = []
+                    nc.vector.quantize_mx(
+                        out=m_codes[:, h, :].bitcast(FP8X4),
+                        scales=m_scales[:, h, :],
+                        in_=m_grouped[:].rearrange("q s j -> q (s j)"),
+                    )
+                if g == 0:
+                    for h in range(H):
+                        regroup_head(0, h)
+                    quantise_p(0)
+
+            for b2 in range(PAIR):
+                own = slice(b2 * HD, (b2 + 1) * HD)
+                other = slice((1 - b2) * HD, (2 - b2) * HD)
+                w_grouped = setup.tile([P, PARITIES, E, PACK], BF16, align_bytes=64, name="w_grouped%d" % b2)
+                nc.gpsimd.memset(w_grouped[other], 0.0)
+                nc.scalar.copy(out=w_grouped[own], in_=w_raw[own].rearrange("q g j n -> q g n j"))
+                for g in range(PARITIES):
+                    nc.vector.quantize_mx(
+                        out=w_codes[b2][:, g, :].bitcast(FP8X4),
+                        scales=w_scales[b2][:, g, :],
+                        in_=w_grouped[:, g].rearrange("q n j -> q (n j)"),
+                    )
+
+        late = ctx.enter_context(tc.tile_pool(name="late", bufs=2))
+
+        def mix_step(bp, u):
+            g, i = divmod(u, N_TILES)
+            if i == 0:
+                c_grouped[bp, g] = stream.tile([P, T, PACK], BF16, align_bytes=64, name="c_grouped%d" % g)
+            codes, scales = p_mx[bp]
+            s_cols = slice(i * TILE, (i + 1) * TILE)
+            mixed = psum.tile([P, PACK, TILE], F32, name="mixed", bufs=3)
+            for j in range(PACK):
+                h = PARITIES * j + g
+                h_cols = slice(h * PAIR * HD, (h + 1) * PAIR * HD)
+                nc.tensor.matmul_mx(
+                    out=mixed[:, j, :],
+                    lhsT=codes[:, h_cols].bitcast(FP8X4),
+                    lhsT_scale=scales[:, h_cols],
+                    rhs=m_codes[:, h, s_cols].bitcast(FP8X4),
+                    rhs_scale=m_scales[:, h, s_cols],
+                    start=True,
+                    stop=True,
+                )
+            nc.vector.tensor_tensor(
+                out=c_grouped[bp, g][:, s_cols, :],
+                in0=mixed[:].rearrange("q j s -> q s j"),
+                in1=mix_b_all[:, g:H:PARITIES, s_cols].rearrange("q j s -> q s j"),
+                op=ALU.add,
+            )
+
+        def quantise_c(bp):
             for g in range(PARITIES):
                 codes = stream.tile([P, T], U32, align_bytes=64, name="c_codes%d" % g)
                 scales = stream.tile([P, T], U8, align_bytes=64, name="c_scales%d" % g)
                 nc.vector.quantize_mx(
                     out=codes[:].bitcast(FP8X4),
                     scales=scales[:],
-                    in_=c_grouped[g][:].rearrange("q s j -> q (s j)"),
+                    in_=c_grouped[bp, g][:].rearrange("q s j -> q (s j)"),
                 )
-                c_codes.append(codes)
-                c_scales.append(scales)
-            return c_codes, c_scales
+                c_mx[bp, g] = (codes, scales)
 
-        def project_pair(bp, c_codes, c_scales, resid):
-            for b2 in range(PAIR):
-                for i in range(N_S_TILES):
-                    s_cols = slice(i * S_TILE, (i + 1) * S_TILE)
-                    y = y_psum.tile([P, E], F32, name="y")
-                    for g in range(PARITIES):
-                        nc.tensor.matmul_mx(
-                            out=y[:],
-                            lhsT=c_codes[g][:, s_cols].bitcast(FP8X4),
-                            lhsT_scale=c_scales[g][:, s_cols],
-                            rhs=w_codes[b2][:, g, :].bitcast(FP8X4),
-                            rhs_scale=w_scales[b2][:, g, :],
-                            start=(g == 0),
-                            stop=(g == PARITIES - 1),
-                        )
-                    nc.vector.tensor_tensor(out=resid[:, b2, i, :], in0=y[:], in1=resid[:, b2, i, :], op=ALU.add)
-                nc.sync.dma_start(
-                    out=out[PAIR * bp + b2].rearrange("(i r) n -> r i n", r=S_TILE),
-                    in_=resid[:, b2],
+        def project_step(bp, u):
+            b2, k = divmod(u, N_TILES)
+            if k == 0:
+                y_t[bp, b2] = late.tile([P, N_TILES, T], F32, name="y_t", bufs=4)
+            n_cols = slice(k * TILE, (k + 1) * TILE)
+            acc = psum.tile([P, T], F32, name="acc", bufs=2)
+            for g in range(PARITIES):
+                codes, scales = c_mx[bp, g]
+                nc.tensor.matmul_mx(
+                    out=acc[:],
+                    lhsT=w_codes[b2][:, g, n_cols].bitcast(FP8X4),
+                    lhsT_scale=w_scales[b2][:, g, n_cols],
+                    rhs=codes[:].bitcast(FP8X4),
+                    rhs_scale=scales[:],
+                    start=(g == 0),
+                    stop=(g == PARITIES - 1),
+                )
+            nc.scalar.activation(out=y_t[bp, b2][:, k, :], in_=acc[:], func=ACT.Identity, bias=out_b_col[:, k : k + 1])
+
+        def finish_step(bp, u):
+            b2, i = divmod(u, N_TILES)
+            if i == 0:
+                y_rows[bp, b2] = late.tile([P, N_TILES, E], F32, name="y_rows", bufs=3)
+            y = psum.tile([P, E], F32, name="y", bufs=3)
+            for k in range(N_TILES):
+                nc.tensor.transpose(
+                    y[:, k * TILE : (k + 1) * TILE], y_t[bp, b2][:, k, i * TILE : (i + 1) * TILE], identity[:]
+                )
+            nc.vector.tensor_tensor(out=y_rows[bp, b2][:, i, :], in0=y[:], in1=x_rows[bp][:, b2, i, :], op=ALU.add)
+            if i == N_TILES - 1:
+                nc.gpsimd.dma_start(
+                    out=out[PAIR * bp + b2].rearrange("(i r) n -> r i n", r=TILE), in_=y_rows[bp, b2][:]
                 )
 
-        prepared = {0: prepare_pair(*loaded[0])}
-        for bp in range(N_PAIRS):
-            if bp + 1 < N_PAIRS:
-                loaded[bp + 1] = load_pair(bp + 1)
-            p_codes, p_scales, resid = prepared[bp]
-            c_codes, c_scales = mix_pair(p_codes, p_scales)
-            if bp + 1 < N_PAIRS:
-                prepared[bp + 1] = prepare_pair(*loaded[bp + 1])
-            project_pair(bp, c_codes, c_scales, resid)
+        for it in range(N_PAIRS + 2):
+            if it + 2 < N_PAIRS:
+                load_p(it + 2)
+            if it < N_PAIRS:
+                load_x(it)
+            for u in range(STEPS):
+                if it < N_PAIRS:
+                    mix_step(it, u)
+                if 0 <= it - 1 < N_PAIRS:
+                    project_step(it - 1, u)
+                if 0 <= it - 2 < N_PAIRS:
+                    finish_step(it - 2, u)
+                if it + 1 < N_PAIRS:
+                    regroup_head(it + 1, u)
+            if it + 1 < N_PAIRS:
+                quantise_p(it + 1)
+            if it < N_PAIRS:
+                quantise_c(it)

@@ -23,6 +23,7 @@ PARITIES = 2
 TILE = 128
 N_TILES = T // TILE
 STEPS = PAIR * N_TILES
+BUNCH = 2
 
 FLOPS = 2 * B * H * T * T * HD + 2 * B * T * E * E
 
@@ -34,7 +35,7 @@ def tile_mixerblock_pa_t_kernel(tc, p, mix_w, mix_b, decay, out_w, out_b, x, out
         stream = ctx.enter_context(tc.tile_pool(name="stream", bufs=2))
         psum = ctx.enter_context(tc.psum_pool(name="psum", bufs=2))
 
-        p_raw, x_rows, p_grouped, p_mx, c_grouped, c_mx, y_t, y_rows = {}, {}, {}, {}, {}, {}, {}, {}
+        p_raw, x_rows, p_grouped, p_mx, c_grouped, c_mx, y_t, y_turned, y_rows = {}, {}, {}, {}, {}, {}, {}, {}, {}
 
         def load_p(bp):
             p_raw[bp] = stream.tile([P, PAIR, H, PACK * HD], BF16, name="p_raw")
@@ -50,33 +51,10 @@ def tile_mixerblock_pa_t_kernel(tc, p, mix_w, mix_b, decay, out_w, out_b, x, out
                     out=x_rows[bp][:, b2], in_=x[PAIR * bp + b2].rearrange("(i r) n -> r i n", r=TILE)
                 )
 
-        load_p(0)
-
-        decay_raw = const.tile([P, H], BF16)
-        nc.sync.dma_start(out=decay_raw[:], in_=decay.partition_broadcast(P))
-        w_rows = const.tile([P, HALF, PACK], BF16)
-        out_b_raw = const.tile([P, N_TILES], BF16)
-        with nc.allow_non_contiguous_dma(reason="two small vectors, spread over the partitions once"):
-            nc.sync.dma_start(out=w_rows[:], in_=mix_w[HALF:H, :].rearrange("h (q j) -> q h j", j=PACK))
-            nc.sync.dma_start(out=out_b_raw[:], in_=out_b.rearrange("(k n) -> n k", n=TILE))
-        out_b_col = const.tile([P, N_TILES], F32)
-        nc.vector.tensor_copy(out=out_b_col[:], in_=out_b_raw[:])
-        mix_b_all = const.tile([P, H, T], BF16)
-        identity = const.tile([P, P], F32)
-        make_identity(nc, identity[:])
-
-        m_codes = const.tile([P, H, T], U32, align_bytes=64)
-        m_scales = const.tile([P, H, T], U8, align_bytes=64)
-        w_codes = [const.tile([P, PARITIES, E], U32, align_bytes=64, name="w_codes%d" % b2) for b2 in range(PAIR)]
-        w_scales = [const.tile([P, PARITIES, E], U8, align_bytes=64, name="w_scales%d" % b2) for b2 in range(PAIR)]
-
-        def regroup_head(bp, h):
+        def regroup_head(bp, h, copy):
             if h == 0:
                 p_grouped[bp] = stream.tile([P, H, PAIR, HD, PACK], BF16, align_bytes=64, name="p_grouped")
-            nc.scalar.copy(
-                out=p_grouped[bp][:, h],
-                in_=p_raw[bp][:, :, h, :].rearrange("q b (j f) -> q b f j", j=PACK),
-            )
+            copy(out=p_grouped[bp][:, h], in_=p_raw[bp][:, :, h, :].rearrange("q b (j f) -> q b f j", j=PACK))
 
         def quantise_p(bp):
             codes = stream.tile([P, H * PAIR * HD], U32, align_bytes=64, name="p_codes")
@@ -88,12 +66,33 @@ def tile_mixerblock_pa_t_kernel(tc, p, mix_w, mix_b, decay, out_w, out_b, x, out
             )
             p_mx[bp] = (codes, scales)
 
+        decay_raw = const.tile([P, H], BF16)
+        nc.sync.dma_start(out=decay_raw[:], in_=decay.partition_broadcast(P))
+        w_rows = const.tile([P, HALF, PACK], BF16)
+        out_b_raw = const.tile([P, N_TILES], BF16)
+        with nc.allow_non_contiguous_dma(reason="two small vectors, spread over the partitions once"):
+            nc.sync.dma_start(out=w_rows[:], in_=mix_w[HALF:H, :].rearrange("h (q j) -> q h j", j=PACK))
+            nc.sync.dma_start(out=out_b_raw[:], in_=out_b.rearrange("(k n) -> n k", n=TILE))
+        load_p(0)
+        mix_b_all = const.tile([P, H, T], BF16)
+        m_codes = const.tile([P, H, T], U32, align_bytes=64)
+        m_scales = const.tile([P, H, T], U8, align_bytes=64)
+        w_codes = [const.tile([P, PARITIES, E], U32, align_bytes=64, name="w_codes%d" % b2) for b2 in range(PAIR)]
+        w_scales = [const.tile([P, PARITIES, E], U8, align_bytes=64, name="w_scales%d" % b2) for b2 in range(PAIR)]
+        identity = const.tile([P, P], F32)
+        out_b_col = const.tile([P, N_TILES], F32)
+
         with tc.tile_pool(name="setup", bufs=1) as setup:
             w_cols = setup.tile([P, HALF, T], BF16)
             nc.sync.dma_start(
                 out=w_cols[:].rearrange("q h s -> q (h s)"),
                 in_=mix_w[0:HALF, :].rearrange("h s -> (h s)").partition_broadcast(P),
             )
+            nc.sync.dma_start(
+                out=mix_b_all[:].rearrange("q h s -> q (h s)"),
+                in_=mix_b.rearrange("h s -> (h s)").partition_broadcast(P),
+            )
+            load_p(1)
             w_raw = setup.tile([P, PARITIES, PACK, E], BF16)
             for b2 in range(PAIR):
                 for g in range(PARITIES):
@@ -101,16 +100,11 @@ def tile_mixerblock_pa_t_kernel(tc, p, mix_w, mix_b, decay, out_w, out_b, x, out
                         out=w_raw[b2 * HD : (b2 + 1) * HD, g],
                         in_=out_w.rearrange("(j g f) n -> g f j n", g=PARITIES, f=HD)[g],
                     )
-            nc.sync.dma_start(
-                out=mix_b_all[:].rearrange("q h s -> q (h s)"),
-                in_=mix_b.rearrange("h s -> (h s)").partition_broadcast(P),
-            )
-            load_p(1)
 
-            s_int = setup.tile([P, T], I32)
-            nc.gpsimd.iota(s_int[:], pattern=[[1, T]], base=0, channel_multiplier=0)
             t_int = setup.tile([P, PACK], I32)
             nc.gpsimd.iota(t_int[:], pattern=[[1, PACK]], base=0, channel_multiplier=PACK)
+            s_int = setup.tile([P, T], I32)
+            nc.gpsimd.iota(s_int[:], pattern=[[1, T]], base=0, channel_multiplier=0)
             causal = setup.tile([P, PACK, T], F32)
             nc.gpsimd.memset(causal[:], 1.0)
             nc.gpsimd.affine_select(
@@ -122,11 +116,17 @@ def tile_mixerblock_pa_t_kernel(tc, p, mix_w, mix_b, decay, out_w, out_b, x, out
                 base=0,
                 channel_multiplier=-PACK,
             )
-            s_idx = setup.tile([P, T], F32)
-            nc.vector.tensor_copy(out=s_idx[:], in_=s_int[:])
+            make_identity(nc, identity[:])
+
+            one = setup.tile([P, 1], F32)
+            nc.vector.memset(one[:], 1.0)
+            warm = setup.tile([P, 1], F32)
+            nc.scalar.activation(out=warm[:], in_=one[:], func=ACT.Ln)
+
             t_idx = setup.tile([P, PACK], F32)
             nc.vector.tensor_copy(out=t_idx[:], in_=t_int[:])
-
+            s_idx = setup.tile([P, T], F32)
+            nc.vector.tensor_copy(out=s_idx[:], in_=s_int[:])
             d = setup.tile([P, H], F32)
             nc.vector.tensor_scalar(
                 out=d[:], in0=decay_raw[:], scalar1=0.9, scalar2=1.0, op0=ALU.max, op1=ALU.min
@@ -147,15 +147,20 @@ def tile_mixerblock_pa_t_kernel(tc, p, mix_w, mix_b, decay, out_w, out_b, x, out
                 out=row_fac[:, HALF:H, :], in0=row_fac[:, HALF:H, :], in1=w_rows[:], op=ALU.mult
             )
 
-            col_fac = setup.tile([P, H, T], F32)
             for h in range(H):
-                nc.scalar.activation(out=col_fac[:, h, :], in_=s_idx[:], func=ACT.Exp, scale=ln_d[:, h : h + 1])
-            nc.vector.tensor_tensor(
-                out=col_fac[:, 0:HALF, :], in0=col_fac[:, 0:HALF, :], in1=w_cols[:], op=ALU.mult
-            )
+                regroup_head(0, h, nc.vector.tensor_copy)
+            quantise_p(0)
 
+            col_fac = setup.tile([P, H, T], F32)
             for g in range(PARITIES):
                 for h in range(g, H, PARITIES):
+                    nc.scalar.activation(
+                        out=col_fac[:, h, :], in_=s_idx[:], func=ACT.Exp, scale=ln_d[:, h : h + 1]
+                    )
+                    if h < HALF:
+                        nc.vector.tensor_tensor(
+                            out=col_fac[:, h, :], in0=col_fac[:, h, :], in1=w_cols[:, h, :], op=ALU.mult
+                        )
                     row_masked = setup.tile([P, PACK, T], F32, name="row_masked", bufs=2)
                     for j in range(PACK):
                         nc.scalar.activation(
@@ -173,11 +178,8 @@ def tile_mixerblock_pa_t_kernel(tc, p, mix_w, mix_b, decay, out_w, out_b, x, out
                         scales=m_scales[:, h, :],
                         in_=m_grouped[:].rearrange("q s j -> q (s j)"),
                     )
-                if g == 0:
-                    for h in range(H):
-                        regroup_head(0, h)
-                    quantise_p(0)
 
+            nc.vector.tensor_copy(out=out_b_col[:], in_=out_b_raw[:])
             for b2 in range(PAIR):
                 own = slice(b2 * HD, (b2 + 1) * HD)
                 other = slice((1 - b2) * HD, (2 - b2) * HD)
@@ -199,7 +201,7 @@ def tile_mixerblock_pa_t_kernel(tc, p, mix_w, mix_b, decay, out_w, out_b, x, out
                 c_grouped[bp, g] = stream.tile([P, T, PACK], BF16, align_bytes=64, name="c_grouped%d" % g)
             codes, scales = p_mx[bp]
             s_cols = slice(i * TILE, (i + 1) * TILE)
-            mixed = psum.tile([P, PACK, TILE], F32, name="mixed", bufs=3)
+            mixed = psum.tile([P, PACK, TILE], F32, name="mixed", bufs=2)
             for j in range(PACK):
                 h = PARITIES * j + g
                 h_cols = slice(h * PAIR * HD, (h + 1) * PAIR * HD)
@@ -249,36 +251,53 @@ def tile_mixerblock_pa_t_kernel(tc, p, mix_w, mix_b, decay, out_w, out_b, x, out
                 )
             nc.scalar.activation(out=y_t[bp, b2][:, k, :], in_=acc[:], func=ACT.Identity, bias=out_b_col[:, k : k + 1])
 
-        def finish_step(bp, u):
+        def turn_back(bp, u):
             b2, i = divmod(u, N_TILES)
-            if i == 0:
-                y_rows[bp, b2] = late.tile([P, N_TILES, E], F32, name="y_rows", bufs=3)
-            y = psum.tile([P, E], F32, name="y", bufs=3)
+            y = psum.tile([P, E], F32, name="y", bufs=4)
             for k in range(N_TILES):
                 nc.tensor.transpose(
                     y[:, k * TILE : (k + 1) * TILE], y_t[bp, b2][:, k, i * TILE : (i + 1) * TILE], identity[:]
                 )
-            nc.vector.tensor_tensor(out=y_rows[bp, b2][:, i, :], in0=y[:], in1=x_rows[bp][:, b2, i, :], op=ALU.add)
+            y_turned[bp, u] = y
+
+        def add_x(bp, u):
+            b2, i = divmod(u, N_TILES)
+            if i == 0:
+                y_rows[bp, b2] = late.tile([P, N_TILES, E], F32, name="y_rows", bufs=3)
+            nc.vector.tensor_tensor(
+                out=y_rows[bp, b2][:, i, :], in0=y_turned[bp, u][:], in1=x_rows[bp][:, b2, i, :], op=ALU.add
+            )
             if i == N_TILES - 1:
                 nc.gpsimd.dma_start(
                     out=out[PAIR * bp + b2].rearrange("(i r) n -> r i n", r=TILE), in_=y_rows[bp, b2][:]
                 )
 
-        for it in range(N_PAIRS + 2):
-            if it + 2 < N_PAIRS:
-                load_p(it + 2)
-            if it < N_PAIRS:
-                load_x(it)
-            for u in range(STEPS):
+        with tc.manual_schedule():
+            turned = []
+            for it in range(N_PAIRS + 2):
+                if it + 2 < N_PAIRS:
+                    load_p(it + 2)
                 if it < N_PAIRS:
-                    mix_step(it, u)
-                if 0 <= it - 1 < N_PAIRS:
-                    project_step(it - 1, u)
-                if 0 <= it - 2 < N_PAIRS:
-                    finish_step(it - 2, u)
+                    load_x(it)
+                for first in range(0, STEPS, BUNCH):
+                    bunch = range(first, first + BUNCH)
+                    if it + 1 < N_PAIRS:
+                        for u in bunch:
+                            regroup_head(it + 1, u, nc.scalar.copy)
+                    if it < N_PAIRS:
+                        for u in bunch:
+                            mix_step(it, u)
+                    if 0 <= it - 1 < N_PAIRS:
+                        for u in bunch:
+                            project_step(it - 1, u)
+                    for bp, u in turned:
+                        add_x(bp, u)
+                    turned = [(it - 2, u) for u in bunch] if 0 <= it - 2 < N_PAIRS else []
+                    for bp, u in turned:
+                        turn_back(bp, u)
                 if it + 1 < N_PAIRS:
-                    regroup_head(it + 1, u)
-            if it + 1 < N_PAIRS:
-                quantise_p(it + 1)
-            if it < N_PAIRS:
-                quantise_c(it)
+                    quantise_p(it + 1)
+                if it < N_PAIRS:
+                    quantise_c(it)
+            for bp, u in turned:
+                add_x(bp, u)

@@ -24,6 +24,7 @@ TILE = 128
 N_TILES = T // TILE
 STEPS = PAIR * N_TILES
 BUNCH = 2
+BY_VECTOR = 1
 
 FLOPS = 2 * B * H * T * T * HD + 2 * B * T * E * E
 
@@ -69,11 +70,8 @@ def tile_mixerblock_pa_t_kernel(tc, p, mix_w, mix_b, decay, out_w, out_b, x, out
         decay_raw = const.tile([P, H], BF16)
         nc.sync.dma_start(out=decay_raw[:], in_=decay.partition_broadcast(P))
         w_rows = const.tile([P, HALF, PACK], BF16)
-        out_b_raw = const.tile([P, N_TILES], BF16)
-        with nc.allow_non_contiguous_dma(reason="two small vectors, spread over the partitions once"):
+        with nc.allow_non_contiguous_dma(reason="four neighbouring weights to a partition, once"):
             nc.sync.dma_start(out=w_rows[:], in_=mix_w[HALF:H, :].rearrange("h (q j) -> q h j", j=PACK))
-            nc.sync.dma_start(out=out_b_raw[:], in_=out_b.rearrange("(k n) -> n k", n=TILE))
-        load_p(0)
         mix_b_all = const.tile([P, H, T], BF16)
         m_codes = const.tile([P, H, T], U32, align_bytes=64)
         m_scales = const.tile([P, H, T], U8, align_bytes=64)
@@ -83,6 +81,14 @@ def tile_mixerblock_pa_t_kernel(tc, p, mix_w, mix_b, decay, out_w, out_b, x, out
         out_b_col = const.tile([P, N_TILES], F32)
 
         with tc.tile_pool(name="setup", bufs=1) as setup:
+            w_raw = setup.tile([P, PARITIES, PACK, E], BF16)
+            for b2 in range(PAIR):
+                for g in range(PARITIES):
+                    nc.sync.dma_start(
+                        out=w_raw[b2 * HD : (b2 + 1) * HD, g],
+                        in_=out_w.rearrange("(j g f) n -> g f j n", g=PARITIES, f=HD)[g],
+                    )
+            load_p(0)
             w_cols = setup.tile([P, HALF, T], BF16)
             nc.sync.dma_start(
                 out=w_cols[:].rearrange("q h s -> q (h s)"),
@@ -93,20 +99,16 @@ def tile_mixerblock_pa_t_kernel(tc, p, mix_w, mix_b, decay, out_w, out_b, x, out
                 in_=mix_b.rearrange("h s -> (h s)").partition_broadcast(P),
             )
             load_p(1)
-            w_raw = setup.tile([P, PARITIES, PACK, E], BF16)
-            for b2 in range(PAIR):
-                for g in range(PARITIES):
-                    nc.sync.dma_start(
-                        out=w_raw[b2 * HD : (b2 + 1) * HD, g],
-                        in_=out_w.rearrange("(j g f) n -> g f j n", g=PARITIES, f=HD)[g],
-                    )
+            out_b_raw = setup.tile([P, N_TILES], BF16)
+            with nc.allow_non_contiguous_dma(reason="one value of out_b to a partition, once"):
+                nc.sync.dma_start(out=out_b_raw[:], in_=out_b.rearrange("(k n) -> n k", n=TILE))
 
             t_int = setup.tile([P, PACK], I32)
             nc.gpsimd.iota(t_int[:], pattern=[[1, PACK]], base=0, channel_multiplier=PACK)
             s_int = setup.tile([P, T], I32)
             nc.gpsimd.iota(s_int[:], pattern=[[1, T]], base=0, channel_multiplier=0)
             causal = setup.tile([P, PACK, T], F32)
-            nc.gpsimd.memset(causal[:], 1.0)
+            nc.vector.memset(causal[:], 1.0)
             nc.gpsimd.affine_select(
                 out=causal[:],
                 in_=causal[:],
@@ -147,13 +149,26 @@ def tile_mixerblock_pa_t_kernel(tc, p, mix_w, mix_b, decay, out_w, out_b, x, out
                 out=row_fac[:, HALF:H, :], in0=row_fac[:, HALF:H, :], in1=w_rows[:], op=ALU.mult
             )
 
-            for h in range(H):
-                regroup_head(0, h, nc.vector.tensor_copy)
-            quantise_p(0)
+            w_grouped = setup.tile([P, PARITIES, E, PACK], BF16, align_bytes=64)
+            nc.vector.tensor_copy(out=w_grouped[:], in_=w_raw[:].rearrange("q g j n -> q g n j"))
+            for b2 in range(PAIR):
+                for g in range(PARITIES):
+                    nc.vector.quantize_mx(
+                        out=w_codes[b2][:, g, :].bitcast(FP8X4),
+                        scales=w_scales[b2][:, g, :],
+                        in_=w_grouped[:, g].rearrange("q n j -> q (n j)"),
+                    )
+                nc.vector.memset(w_codes[b2][(1 - b2) * HD : (2 - b2) * HD].bitcast(I32), 0)
+            nc.vector.tensor_copy(out=out_b_col[:], in_=out_b_raw[:])
+
+            for bp in range(BY_VECTOR):
+                for h in range(H):
+                    regroup_head(bp, h, nc.vector.tensor_copy)
+                quantise_p(bp)
 
             col_fac = setup.tile([P, H, T], F32)
             for g in range(PARITIES):
-                for h in range(g, H, PARITIES):
+                for h in range(H - PARITIES + g, -1, -PARITIES):
                     nc.scalar.activation(
                         out=col_fac[:, h, :], in_=s_idx[:], func=ACT.Exp, scale=ln_d[:, h : h + 1]
                     )
@@ -179,20 +194,6 @@ def tile_mixerblock_pa_t_kernel(tc, p, mix_w, mix_b, decay, out_w, out_b, x, out
                         in_=m_grouped[:].rearrange("q s j -> q (s j)"),
                     )
 
-            nc.vector.tensor_copy(out=out_b_col[:], in_=out_b_raw[:])
-            for b2 in range(PAIR):
-                own = slice(b2 * HD, (b2 + 1) * HD)
-                other = slice((1 - b2) * HD, (2 - b2) * HD)
-                w_grouped = setup.tile([P, PARITIES, E, PACK], BF16, align_bytes=64, name="w_grouped%d" % b2)
-                nc.gpsimd.memset(w_grouped[other], 0.0)
-                nc.scalar.copy(out=w_grouped[own], in_=w_raw[own].rearrange("q g j n -> q g n j"))
-                for g in range(PARITIES):
-                    nc.vector.quantize_mx(
-                        out=w_codes[b2][:, g, :].bitcast(FP8X4),
-                        scales=w_scales[b2][:, g, :],
-                        in_=w_grouped[:, g].rearrange("q n j -> q (n j)"),
-                    )
-
         late = ctx.enter_context(tc.tile_pool(name="late", bufs=2))
 
         def mix_step(bp, u):
@@ -201,7 +202,7 @@ def tile_mixerblock_pa_t_kernel(tc, p, mix_w, mix_b, decay, out_w, out_b, x, out
                 c_grouped[bp, g] = stream.tile([P, T, PACK], BF16, align_bytes=64, name="c_grouped%d" % g)
             codes, scales = p_mx[bp]
             s_cols = slice(i * TILE, (i + 1) * TILE)
-            mixed = psum.tile([P, PACK, TILE], F32, name="mixed", bufs=2)
+            mixed = psum.tile([P, PACK, TILE], F32, name="mixed", bufs=3)
             for j in range(PACK):
                 h = PARITIES * j + g
                 h_cols = slice(h * PAIR * HD, (h + 1) * PAIR * HD)
@@ -235,7 +236,7 @@ def tile_mixerblock_pa_t_kernel(tc, p, mix_w, mix_b, decay, out_w, out_b, x, out
         def project_step(bp, u):
             b2, k = divmod(u, N_TILES)
             if k == 0:
-                y_t[bp, b2] = late.tile([P, N_TILES, T], F32, name="y_t", bufs=4)
+                y_t[bp, b2] = late.tile([P, N_TILES, T], F32, name="y_t", bufs=3)
             n_cols = slice(k * TILE, (k + 1) * TILE)
             acc = psum.tile([P, T], F32, name="acc", bufs=2)
             for g in range(PARITIES):
@@ -253,7 +254,7 @@ def tile_mixerblock_pa_t_kernel(tc, p, mix_w, mix_b, decay, out_w, out_b, x, out
 
         def turn_back(bp, u):
             b2, i = divmod(u, N_TILES)
-            y = psum.tile([P, E], F32, name="y", bufs=4)
+            y = psum.tile([P, E], F32, name="y", bufs=3)
             for k in range(N_TILES):
                 nc.tensor.transpose(
                     y[:, k * TILE : (k + 1) * TILE], y_t[bp, b2][:, k, i * TILE : (i + 1) * TILE], identity[:]
@@ -262,42 +263,44 @@ def tile_mixerblock_pa_t_kernel(tc, p, mix_w, mix_b, decay, out_w, out_b, x, out
 
         def add_x(bp, u):
             b2, i = divmod(u, N_TILES)
-            if i == 0:
-                y_rows[bp, b2] = late.tile([P, N_TILES, E], F32, name="y_rows", bufs=3)
+            first, k = u - u % BUNCH, u % BUNCH
+            if k == 0:
+                y_rows[bp, first] = late.tile([P, BUNCH, E], F32, name="y_rows", bufs=4)
             nc.vector.tensor_tensor(
-                out=y_rows[bp, b2][:, i, :], in0=y_turned[bp, u][:], in1=x_rows[bp][:, b2, i, :], op=ALU.add
+                out=y_rows[bp, first][:, k, :], in0=y_turned[bp, u][:], in1=x_rows[bp][:, b2, i, :], op=ALU.add
             )
-            if i == N_TILES - 1:
+            if k == BUNCH - 1:
+                rows = slice((i - k) * TILE, (i + 1) * TILE)
                 nc.gpsimd.dma_start(
-                    out=out[PAIR * bp + b2].rearrange("(i r) n -> r i n", r=TILE), in_=y_rows[bp, b2][:]
+                    out=out[PAIR * bp + b2, rows, :].rearrange("(k r) n -> r k n", r=TILE), in_=y_rows[bp, first][:]
                 )
 
-        with tc.manual_schedule():
-            turned = []
-            for it in range(N_PAIRS + 2):
-                if it + 2 < N_PAIRS:
-                    load_p(it + 2)
-                if it < N_PAIRS:
-                    load_x(it)
-                for first in range(0, STEPS, BUNCH):
-                    bunch = range(first, first + BUNCH)
-                    if it + 1 < N_PAIRS:
-                        for u in bunch:
-                            regroup_head(it + 1, u, nc.scalar.copy)
-                    if it < N_PAIRS:
-                        for u in bunch:
-                            mix_step(it, u)
-                    if 0 <= it - 1 < N_PAIRS:
-                        for u in bunch:
-                            project_step(it - 1, u)
-                    for bp, u in turned:
-                        add_x(bp, u)
-                    turned = [(it - 2, u) for u in bunch] if 0 <= it - 2 < N_PAIRS else []
-                    for bp, u in turned:
-                        turn_back(bp, u)
-                if it + 1 < N_PAIRS:
-                    quantise_p(it + 1)
-                if it < N_PAIRS:
-                    quantise_c(it)
-            for bp, u in turned:
-                add_x(bp, u)
+        def steps_behind(it, first, lag):
+            start = it * STEPS + first - lag
+            return [divmod(start + k, STEPS) for k in range(BUNCH) if 0 <= start + k < N_PAIRS * STEPS]
+
+        turned = []
+        for it in range(N_PAIRS + 2):
+            if it + 2 < N_PAIRS:
+                load_p(it + 2)
+            if it < N_PAIRS:
+                load_x(it)
+            for first in range(0, STEPS, BUNCH):
+                for bp, u in steps_behind(it, first, -STEPS):
+                    if bp >= BY_VECTOR:
+                        regroup_head(bp, u, nc.scalar.copy)
+                for bp, u in steps_behind(it, first, 0):
+                    mix_step(bp, u)
+                for bp, u in steps_behind(it, first, STEPS):
+                    project_step(bp, u)
+                for bp, u in turned:
+                    add_x(bp, u)
+                turned = steps_behind(it, first, STEPS + N_TILES)
+                for bp, u in turned:
+                    turn_back(bp, u)
+            if BY_VECTOR <= it + 1 < N_PAIRS:
+                quantise_p(it + 1)
+            if it < N_PAIRS:
+                quantise_c(it)
+        for bp, u in turned:
+            add_x(bp, u)

@@ -271,7 +271,7 @@ def tile_mixerblock_pa_t_kernel(tc, p, mix_w, mix_b, decay, out_w, out_b, x, out
             )
             if k == BUNCH - 1:
                 rows = slice((i - k) * TILE, (i + 1) * TILE)
-                nc.gpsimd.dma_start(
+                nc.sync.dma_start(
                     out=out[PAIR * bp + b2, rows, :].rearrange("(k r) n -> r k n", r=TILE), in_=y_rows[bp, first][:]
                 )
 

from contextlib import ExitStack

import concourse.mybir as mybir
from concourse.masks import make_identity

F32 = mybir.dt.float32
BF16 = mybir.dt.bfloat16
I32 = mybir.dt.int32
U32 = mybir.dt.uint32
U8 = mybir.dt.uint8
FP8X4 = mybir.dt.float8_e4m3fn_x4
ALU = mybir.AluOpType
ACT = mybir.ActivationFunctionType

B, H, T, HD = 16, 8, 512, 64
E = H * HD
HALF = H // 2
P = 128
PACK = 4
PAIR = 2
N_PAIRS = B // PAIR
PARITIES = 2
TILE = 128
N_TILES = T // TILE
STEPS = PAIR * N_TILES
BUNCH = 2
BY_VECTOR = 1

FLOPS = 2 * B * H * T * T * HD + 2 * B * T * E * E


def tile_mixerblock_pa_t_kernel(tc, p, mix_w, mix_b, decay, out_w, out_b, x, out):
    nc = tc.nc
    with ExitStack() as ctx:
        const = ctx.enter_context(tc.tile_pool(name="const", bufs=1))
        stream = ctx.enter_context(tc.tile_pool(name="stream", bufs=2))
        psum = ctx.enter_context(tc.psum_pool(name="psum", bufs=2))

        p_raw, x_rows, p_grouped, p_mx, c_grouped, c_mx, y_t, y_turned, y_rows = {}, {}, {}, {}, {}, {}, {}, {}, {}

        def load_p(bp):
            p_raw[bp] = stream.tile([P, PAIR, H, PACK * HD], BF16, name="p_raw")
            for b2 in range(PAIR):
                nc.sync.dma_start(
                    out=p_raw[bp][:, b2], in_=p[PAIR * bp + b2].rearrange("h (q j) f -> q h (j f)", j=PACK)
                )

        def load_x(bp):
            x_rows[bp] = stream.tile([P, PAIR, N_TILES, E], BF16, name="x_rows", bufs=3)
            for b2 in range(PAIR):
                nc.sync.dma_start(
                    out=x_rows[bp][:, b2], in_=x[PAIR * bp + b2].rearrange("(i r) n -> r i n", r=TILE)
                )

        def regroup_head(bp, h, copy):
            if h == 0:
                p_grouped[bp] = stream.tile([P, H, PAIR, HD, PACK], BF16, align_bytes=64, name="p_grouped")
            copy(out=p_grouped[bp][:, h], in_=p_raw[bp][:, :, h, :].rearrange("q b (j f) -> q b f j", j=PACK))

        def quantise_p(bp):
            codes = stream.tile([P, H * PAIR * HD], U32, align_bytes=64, name="p_codes")
            scales = stream.tile([P, H * PAIR * HD], U8, align_bytes=64, name="p_scales")
            nc.vector.quantize_mx(
                out=codes[:].bitcast(FP8X4),
                scales=scales[:],
                in_=p_grouped[bp][:].rearrange("q h b f j -> q (h b f j)"),
            )
            p_mx[bp] = (codes, scales)

        decay_raw = const.tile([P, H], BF16)
        nc.sync.dma_start(out=decay_raw[:], in_=decay.partition_broadcast(P))
        w_rows = const.tile([P, HALF, PACK], BF16)
        with nc.allow_non_contiguous_dma(reason="four neighbouring weights to a partition, once"):
            nc.sync.dma_start(out=w_rows[:], in_=mix_w[HALF:H, :].rearrange("h (q j) -> q h j", j=PACK))
        mix_b_all = const.tile([P, H, T], BF16)
        m_codes = const.tile([P, H, T], U32, align_bytes=64)
        m_scales = const.tile([P, H, T], U8, align_bytes=64)
        w_codes = [const.tile([P, PARITIES, E], U32, align_bytes=64, name="w_codes%d" % b2) for b2 in range(PAIR)]
        w_scales = [const.tile([P, PARITIES, E], U8, align_bytes=64, name="w_scales%d" % b2) for b2 in range(PAIR)]
        identity = const.tile([P, P], F32)
        out_b_col = const.tile([P, N_TILES], F32)

        with tc.tile_pool(name="setup", bufs=1) as setup:
            w_raw = setup.tile([P, PARITIES, PACK, E], BF16)
            for b2 in range(PAIR):
                for g in range(PARITIES):
                    nc.sync.dma_start(
                        out=w_raw[b2 * HD : (b2 + 1) * HD, g],
                        in_=out_w.rearrange("(j g f) n -> g f j n", g=PARITIES, f=HD)[g],
                    )
            load_p(0)
            w_cols = setup.tile([P, HALF, T], BF16)
            nc.sync.dma_start(
                out=w_cols[:].rearrange("q h s -> q (h s)"),
                in_=mix_w[0:HALF, :].rearrange("h s -> (h s)").partition_broadcast(P),
            )
            nc.sync.dma_start(
                out=mix_b_all[:].rearrange("q h s -> q (h s)"),
                in_=mix_b.rearrange("h s -> (h s)").partition_broadcast(P),
            )
            load_p(1)
            out_b_raw = setup.tile([P, N_TILES], BF16)
            with nc.allow_non_contiguous_dma(reason="one value of out_b to a partition, once"):
                nc.sync.dma_start(out=out_b_raw[:], in_=out_b.rearrange("(k n) -> n k", n=TILE))

            t_int = setup.tile([P, PACK], I32)
            nc.gpsimd.iota(t_int[:], pattern=[[1, PACK]], base=0, channel_multiplier=PACK)
            s_int = setup.tile([P, T], I32)
            nc.gpsimd.iota(s_int[:], pattern=[[1, T]], base=0, channel_multiplier=0)
            causal = setup.tile([P, PACK, T], F32)
            nc.vector.memset(causal[:], 1.0)
            nc.gpsimd.affine_select(
                out=causal[:],
                in_=causal[:],
                pattern=[[-1, PACK], [1, T]],
                compare_op=ALU.is_ge,
                fill=0.0,
                base=0,
                channel_multiplier=-PACK,
            )
            make_identity(nc, identity[:])

            one = setup.tile([P, 1], F32)
            nc.vector.memset(one[:], 1.0)
            warm = setup.tile([P, 1], F32)
            nc.scalar.activation(out=warm[:], in_=one[:], func=ACT.Ln)

            t_idx = setup.tile([P, PACK], F32)
            nc.vector.tensor_copy(out=t_idx[:], in_=t_int[:])
            s_idx = setup.tile([P, T], F32)
            nc.vector.tensor_copy(out=s_idx[:], in_=s_int[:])
            d = setup.tile([P, H], F32)
            nc.vector.tensor_scalar(
                out=d[:], in0=decay_raw[:], scalar1=0.9, scalar2=1.0, op0=ALU.max, op1=ALU.min
            )
            ln_d = setup.tile([P, H], F32)
            nc.scalar.activation(out=ln_d[:], in_=d[:], func=ACT.Ln)

            row_arg = setup.tile([P, H, PACK], F32)
            nc.vector.tensor_tensor(
                out=row_arg[:],
                in0=t_idx[:].unsqueeze(1).to_broadcast([P, H, PACK]),
                in1=ln_d[:].unsqueeze(2).to_broadcast([P, H, PACK]),
                op=ALU.mult,
            )
            row_fac = setup.tile([P, H, PACK], F32)
            nc.scalar.activation(out=row_fac[:], in_=row_arg[:], func=ACT.Exp, scale=-1.0)
            nc.vector.tensor_tensor(
                out=row_fac[:, HALF:H, :], in0=row_fac[:, HALF:H, :], in1=w_rows[:], op=ALU.mult
            )

            w_grouped = setup.tile([P, PARITIES, E, PACK], BF16, align_bytes=64)
            nc.vector.tensor_copy(out=w_grouped[:], in_=w_raw[:].rearrange("q g j n -> q g n j"))
            for b2 in range(PAIR):
                for g in range(PARITIES):
                    nc.vector.quantize_mx(
                        out=w_codes[b2][:, g, :].bitcast(FP8X4),
                        scales=w_scales[b2][:, g, :],
                        in_=w_grouped[:, g].rearrange("q n j -> q (n j)"),
                    )
                nc.vector.memset(w_codes[b2][(1 - b2) * HD : (2 - b2) * HD].bitcast(I32), 0)
            nc.vector.tensor_copy(out=out_b_col[:], in_=out_b_raw[:])

            for bp in range(BY_VECTOR):
                for h in range(H):
                    regroup_head(bp, h, nc.vector.tensor_copy)
                quantise_p(bp)

            col_fac = setup.tile([P, H, T], F32)
            for g in range(PARITIES):
                for h in range(H - PARITIES + g, -1, -PARITIES):
                    nc.scalar.activation(
                        out=col_fac[:, h, :], in_=s_idx[:], func=ACT.Exp, scale=ln_d[:, h : h + 1]
                    )
                    if h < HALF:
                        nc.vector.tensor_tensor(
                            out=col_fac[:, h, :], in0=col_fac[:, h, :], in1=w_cols[:, h, :], op=ALU.mult
                        )
                    row_masked = setup.tile([P, PACK, T], F32, name="row_masked", bufs=2)
                    for j in range(PACK):
                        nc.scalar.activation(
                            out=row_masked[:, j, :], in_=causal[:, j, :], func=ACT.Copy, scale=row_fac[:, h, j : j + 1]
                        )
                    m_grouped = setup.tile([P, T, PACK], BF16, align_bytes=64, name="m_grouped", bufs=2)
                    nc.vector.tensor_tensor(
                        out=m_grouped[:],
                        in0=row_masked[:].rearrange("q j s -> q s j"),
                        in1=col_fac[:, h, :].unsqueeze(2).to_broadcast([P, T, PACK]),
                        op=ALU.mult,
                    )
                    nc.vector.quantize_mx(
                        out=m_codes[:, h, :].bitcast(FP8X4),
                        scales=m_scales[:, h, :],
                        in_=m_grouped[:].rearrange("q s j -> q (s j)"),
                    )

        late = ctx.enter_context(tc.tile_pool(name="late", bufs=2))

        def mix_step(bp, u):
            g, i = divmod(u, N_TILES)
            if i == 0:
                c_grouped[bp, g] = stream.tile([P, T, PACK], BF16, align_bytes=64, name="c_grouped%d" % g)
            codes, scales = p_mx[bp]
            s_cols = slice(i * TILE, (i + 1) * TILE)
            mixed = psum.tile([P, PACK, TILE], F32, name="mixed", bufs=3)
            for j in range(PACK):
                h = PARITIES * j + g
                h_cols = slice(h * PAIR * HD, (h + 1) * PAIR * HD)
                nc.tensor.matmul_mx(
                    out=mixed[:, j, :],
                    lhsT=codes[:, h_cols].bitcast(FP8X4),
                    lhsT_scale=scales[:, h_cols],
                    rhs=m_codes[:, h, s_cols].bitcast(FP8X4),
                    rhs_scale=m_scales[:, h, s_cols],
                    start=True,
                    stop=True,
                )
            nc.vector.tensor_tensor(
                out=c_grouped[bp, g][:, s_cols, :],
                in0=mixed[:].rearrange("q j s -> q s j"),
                in1=mix_b_all[:, g:H:PARITIES, s_cols].rearrange("q j s -> q s j"),
                op=ALU.add,
            )

        def quantise_c(bp):
            for g in range(PARITIES):
                codes = stream.tile([P, T], U32, align_bytes=64, name="c_codes%d" % g)
                scales = stream.tile([P, T], U8, align_bytes=64, name="c_scales%d" % g)
                nc.vector.quantize_mx(
                    out=codes[:].bitcast(FP8X4),
                    scales=scales[:],
                    in_=c_grouped[bp, g][:].rearrange("q s j -> q (s j)"),
                )
                c_mx[bp, g] = (codes, scales)

        def project_step(bp, u):
            b2, k = divmod(u, N_TILES)
            if k == 0:
                y_t[bp, b2] = late.tile([P, N_TILES, T], F32, name="y_t", bufs=3)
            n_cols = slice(k * TILE, (k + 1) * TILE)
            acc = psum.tile([P, T], F32, name="acc", bufs=2)
            for g in range(PARITIES):
                codes, scales = c_mx[bp, g]
                nc.tensor.matmul_mx(
                    out=acc[:],
                    lhsT=w_codes[b2][:, g, n_cols].bitcast(FP8X4),
                    lhsT_scale=w_scales[b2][:, g, n_cols],
                    rhs=codes[:].bitcast(FP8X4),
                    rhs_scale=scales[:],
                    start=(g == 0),
                    stop=(g == PARITIES - 1),
                )
            nc.scalar.activation(out=y_t[bp, b2][:, k, :], in_=acc[:], func=ACT.Identity, bias=out_b_col[:, k : k + 1])

        def turn_back(bp, u):
            b2, i = divmod(u, N_TILES)
            y = psum.tile([P, E], F32, name="y", bufs=3)
            for k in range(N_TILES):
                nc.tensor.transpose(
                    y[:, k * TILE : (k + 1) * TILE], y_t[bp, b2][:, k, i * TILE : (i + 1) * TILE], identity[:]
                )
            y_turned[bp, u] = y

        def add_x(bp, u):
            b2, i = divmod(u, N_TILES)
            first, k = u - u % BUNCH, u % BUNCH
            if k == 0:
                y_rows[bp, first] = late.tile([P, BUNCH, E], F32, name="y_rows", bufs=4)
            nc.vector.tensor_tensor(
                out=y_rows[bp, first][:, k, :], in0=y_turned[bp, u][:], in1=x_rows[bp][:, b2, i, :], op=ALU.add
            )
            if k == BUNCH - 1:
                rows = slice((i - k) * TILE, (i + 1) * TILE)
                nc.sync.dma_start(
                    out=out[PAIR * bp + b2, rows, :].rearrange("(k r) n -> r k n", r=TILE), in_=y_rows[bp, first][:]
                )

        def steps_behind(it, first, lag):
            start = it * STEPS + first - lag
            return [divmod(start + k, STEPS) for k in range(BUNCH) if 0 <= start + k < N_PAIRS * STEPS]

        turned = []
        for it in range(N_PAIRS + 2):
            if it + 2 < N_PAIRS:
                load_p(it + 2)
            if it < N_PAIRS:
                load_x(it)
            for first in range(0, STEPS, BUNCH):
                for bp, u in steps_behind(it, first, -STEPS):
                    if bp >= BY_VECTOR:
                        regroup_head(bp, u, nc.scalar.copy)
                for bp, u in steps_behind(it, first, 0):
                    mix_step(bp, u)
                for bp, u in steps_behind(it, first, STEPS):
                    project_step(bp, u)
                for bp, u in turned:
                    add_x(bp, u)
                turned = steps_behind(it, first, STEPS + N_TILES)
                for bp, u in turned:
                    turn_back(bp, u)
            if BY_VECTOR <= it + 1 < N_PAIRS:
                quantise_p(it + 1)
            if it < N_PAIRS:
                quantise_c(it)
        for bp, u in turned:
            add_x(bp, u)
